import numpy as np
import ml_dtypes

BF16 = ml_dtypes.bfloat16


def bf(x):
    return np.asarray(x, np.float32).astype(BF16)


def f32(x):
    return np.asarray(x, np.float32)


def f64(x):
    return np.asarray(x).astype(np.float64)


def striped(idx):
    return np.tile(idx.reshape(-1, 16).T, (8, 1))


C, E, S, N = 128, 128, 256, 128
EPS = 1e-5


def norm0(v):
    mu = v.mean(axis=0, keepdims=True)
    var = ((v - mu) ** 2).mean(axis=0, keepdims=True)
    return (v - mu) / np.sqrt(var + EPS)


def sigmoid(v):
    return 1.0 / (1.0 + np.exp(-v))


def setup_inputs():
    return {"node": f32(0.5 + 1.5 * np.random.standard_normal((C, N))), "cond": f32(0.5 + 1.5 * np.random.standard_normal((E, S))), "ln_w": f32(1.0 + 0.1 * np.random.standard_normal((E, 1))), "w": bf(np.random.standard_normal((E, C)) / np.sqrt(E)), "b": f32(0.1 * np.random.standard_normal((C, 1))), "offs": striped(np.random.permutation(np.tile(np.arange(S), 2))[:N])}


def reference(node, cond, ln_w, w, b, offs):
    idx = offs[:16].T.reshape(-1)
    sn = norm0(f64(node))
    cn = norm0(f64(cond)) * f64(ln_w)
    tab = sigmoid(f64(w).T @ cn + f64(b))
    return tab[:, idx] * sn

@@ -1,0 +1,73 @@
+import concourse.mybir as mybir
+from concourse.masks import make_identity
+
+F32 = mybir.dt.float32
+BF16 = mybir.dt.bfloat16
+U16 = mybir.dt.uint16
+ACT = mybir.ActivationFunctionType
+MULT = mybir.AluOpType.mult
+
+P = 128
+S = 256
+N = 128
+EPS = 1e-5
+
+FLOPS = 2 * P * P * S
+
+
+def tile_conditionedblockattentionpairbias_kernel(tc, node, cond, ln_w, w, b, offs, out):
+    nc = tc.nc
+    with (
+        tc.tile_pool(name="held", bufs=1) as held,
+        tc.psum_pool(name="psum", bufs=1) as psum,
+    ):
+        cond_sb = held.tile([P, S], F32, name="cond_sb")
+        nc.sync.dma_start(cond_sb[:], cond)
+        node_sb = held.tile([P, N], F32, name="node_sb")
+        nc.scalar.dma_start(node_sb[:], node)
+        offsets = held.tile([P, N // 16], U16, name="offsets")
+        nc.sync.dma_start(offsets[:], offs)
+        w_sb = held.tile([P, P], BF16, name="w_sb")
+        nc.gpsimd.dma_start(w_sb[:], w)
+        ln_w_sb = held.tile([P, 1], F32, name="ln_w_sb")
+        nc.gpsimd.dma_start(ln_w_sb[:], ln_w)
+        b_sb = held.tile([P, 1], F32, name="b_sb")
+        nc.gpsimd.dma_start(b_sb[:], b)
+
+        identity = held.tile([P, P], F32, name="identity")
+        make_identity(nc, identity[:])
+        centre = held.tile([P, P], F32, name="centre")
+        nc.vector.tensor_scalar_add(centre[:], identity[:], -1.0 / P)
+        average = held.tile([P, P], F32, name="average")
+        nc.vector.memset(average[:], 1.0 / P)
+
+        def centred_and_rstd(x_sb, width, name):
+            centred = psum.tile([P, width], F32, name=name + "_centred")
+            nc.tensor.matmul(centred[:], centre[:], x_sb[:], start=True, stop=True)
+            squares = held.tile([P, width], F32, name=name + "_squares")
+            nc.scalar.activation(squares[:], centred[:], ACT.Square)
+            var = psum.tile([P, width], F32, name=name + "_var")
+            nc.tensor.matmul(var[:], average[:], squares[:], start=True, stop=True)
+            std = held.tile([P, width], F32, name=name + "_std")
+            nc.scalar.activation(std[:], var[:], ACT.Sqrt, bias=EPS)
+            rstd = held.tile([P, width], F32, name=name + "_rstd")
+            nc.vector.reciprocal(rstd[:], std[:])
+            return centred, rstd
+
+        cond_centred, cond_rstd = centred_and_rstd(cond_sb, S, "cond")
+        node_centred, node_rstd = centred_and_rstd(node_sb, N, "node")
+
+        cn = held.tile([P, S], BF16, name="cn")
+        nc.vector.scalar_tensor_tensor(cn[:], cond_centred[:], ln_w_sb[:, 0:1], cond_rstd[:], MULT, MULT)
+
+        projected = psum.tile([P, S], F32, name="projected")
+        nc.tensor.matmul(projected[:], w_sb[:], cn[:], start=True, stop=True)
+        tab = held.tile([P, S], F32, name="tab")
+        nc.scalar.activation(tab[:], projected[:], ACT.Sigmoid, bias=b_sb[:, 0:1])
+
+        sn = held.tile([P, N], F32, name="sn")
+        nc.vector.tensor_tensor(sn[:], node_centred[:], node_rstd[:], MULT)
+
+        product = held.tile([P, N], F32, name="product")
+        nc.vector.tensor_tensor(product[:], tab[:].indirect(offsets[:]), sn[:], MULT)
+        nc.sync.dma_start(out, product[:])

@@ -1,5 +1,4 @@
 import concourse.mybir as mybir
-from concourse.masks import make_identity
 
 F32 = mybir.dt.float32
 BF16 = mybir.dt.bfloat16
@@ -25,38 +24,58 @@ def tile_conditionedblockattentionpairbias_kernel(tc, node, cond, ln_w, w, b, of
         nc.sync.dma_start(cond_sb[:], cond)
         node_sb = held.tile([P, N], F32, name="node_sb")
         nc.scalar.dma_start(node_sb[:], node)
+        ln_w_sb = held.tile([P, 1], F32, name="ln_w_sb")
+        nc.sync.dma_start(ln_w_sb[:], ln_w)
+        w_sb = held.tile([P, P], BF16, name="w_sb")
+        nc.scalar.dma_start(w_sb[:], w)
+        b_sb = held.tile([P, 1], F32, name="b_sb")
+        nc.sync.dma_start(b_sb[:], b)
         offsets = held.tile([P, N // 16], U16, name="offsets")
         nc.sync.dma_start(offsets[:], offs)
-        w_sb = held.tile([P, P], BF16, name="w_sb")
-        nc.gpsimd.dma_start(w_sb[:], w)
-        ln_w_sb = held.tile([P, 1], F32, name="ln_w_sb")
-        nc.gpsimd.dma_start(ln_w_sb[:], ln_w)
-        b_sb = held.tile([P, 1], F32, name="b_sb")
-        nc.gpsimd.dma_start(b_sb[:], b)
 
-        identity = held.tile([P, P], F32, name="identity")
-        make_identity(nc, identity[:])
         centre = held.tile([P, P], F32, name="centre")
-        nc.vector.tensor_scalar_add(centre[:], identity[:], -1.0 / P)
+        nc.gpsimd.memset(centre[:], -1.0 / P)
+        nc.gpsimd.affine_select(
+            out=centre[:],
+            in_=centre[:],
+            pattern=[[-1, P]],
+            compare_op=mybir.AluOpType.not_equal,
+            fill=1.0 - 1.0 / P,
+            base=0,
+            channel_multiplier=1,
+        )
         average = held.tile([P, P], F32, name="average")
         nc.vector.memset(average[:], 1.0 / P)
 
-        def centred_and_rstd(x_sb, width, name):
+        scratch = held.tile([P, 1], F32, name="scratch")
+        nc.vector.memset(scratch[:], 1.0)
+        scratch_sqrt = held.tile([P, 1], F32, name="scratch_sqrt")
+        nc.scalar.activation(scratch_sqrt[:], scratch[:], ACT.Sqrt)
+
+        def centred_squares(x_sb, width, name):
             centred = psum.tile([P, width], F32, name=name + "_centred")
             nc.tensor.matmul(centred[:], centre[:], x_sb[:], start=True, stop=True)
             squares = held.tile([P, width], F32, name=name + "_squares")
             nc.scalar.activation(squares[:], centred[:], ACT.Square)
+            return centred, squares
+
+        def standard_deviation(squares, width, name):
             var = psum.tile([P, width], F32, name=name + "_var")
             nc.tensor.matmul(var[:], average[:], squares[:], start=True, stop=True)
             std = held.tile([P, width], F32, name=name + "_std")
             nc.scalar.activation(std[:], var[:], ACT.Sqrt, bias=EPS)
-            rstd = held.tile([P, width], F32, name=name + "_rstd")
-            nc.vector.reciprocal(rstd[:], std[:])
-            return centred, rstd
+            return std
 
-        cond_centred, cond_rstd = centred_and_rstd(cond_sb, S, "cond")
-        node_centred, node_rstd = centred_and_rstd(node_sb, N, "node")
+        cond_centred, cond_squares = centred_squares(cond_sb, S, "cond")
+        node_centred, node_squares = centred_squares(node_sb, N, "node")
+        cond_std = standard_deviation(cond_squares, S, "cond")
+        node_std = standard_deviation(node_squares, N, "node")
 
+        scratch_sigmoid = held.tile([P, 1], F32, name="scratch_sigmoid")
+        nc.scalar.activation(scratch_sigmoid[:], node_std[:, 0:1], ACT.Sigmoid)
+
+        cond_rstd = held.tile([P, S], F32, name="cond_rstd")
+        nc.vector.reciprocal(cond_rstd[:], cond_std[:])
         cn = held.tile([P, S], BF16, name="cn")
         nc.vector.scalar_tensor_tensor(cn[:], cond_centred[:], ln_w_sb[:, 0:1], cond_rstd[:], MULT, MULT)
 
@@ -65,6 +84,8 @@ def tile_conditionedblockattentionpairbias_kernel(tc, node, cond, ln_w, w, b, of
         tab = held.tile([P, S], F32, name="tab")
         nc.scalar.activation(tab[:], projected[:], ACT.Sigmoid, bias=b_sb[:, 0:1])
 
+        node_rstd = held.tile([P, N], F32, name="node_rstd")
+        nc.vector.reciprocal(node_rstd[:], node_std[:])
         sn = held.tile([P, N], F32, name="sn")
         nc.vector.tensor_tensor(sn[:], node_centred[:], node_rstd[:], MULT)
 

@@ -49,8 +49,8 @@ def tile_conditionedblockattentionpairbias_kernel(tc, node, cond, ln_w, w, b, of
 
         scratch = held.tile([P, 1], F32, name="scratch")
         nc.vector.memset(scratch[:], 1.0)
-        scratch_sqrt = held.tile([P, 1], F32, name="scratch_sqrt")
-        nc.scalar.activation(scratch_sqrt[:], scratch[:], ACT.Sqrt)
+        scratch_rsqrt = held.tile([P, 1], F32, name="scratch_rsqrt")
+        nc.scalar.activation(scratch_rsqrt[:], scratch[:], ACT.Abs_reciprocal_sqrt)
 
         def centred_squares(x_sb, width, name):
             centred = psum.tile([P, width], F32, name=name + "_centred")
@@ -59,23 +59,21 @@ def tile_conditionedblockattentionpairbias_kernel(tc, node, cond, ln_w, w, b, of
             nc.scalar.activation(squares[:], centred[:], ACT.Square)
             return centred, squares
 
-        def standard_deviation(squares, width, name):
+        def reciprocal_std(squares, width, name):
             var = psum.tile([P, width], F32, name=name + "_var")
             nc.tensor.matmul(var[:], average[:], squares[:], start=True, stop=True)
-            std = held.tile([P, width], F32, name=name + "_std")
-            nc.scalar.activation(std[:], var[:], ACT.Sqrt, bias=EPS)
-            return std
+            rstd = held.tile([P, width], F32, name=name + "_rstd")
+            nc.scalar.activation(rstd[:], var[:], ACT.Abs_reciprocal_sqrt, bias=EPS)
+            return rstd
 
         cond_centred, cond_squares = centred_squares(cond_sb, S, "cond")
         node_centred, node_squares = centred_squares(node_sb, N, "node")
-        cond_std = standard_deviation(cond_squares, S, "cond")
-        node_std = standard_deviation(node_squares, N, "node")
+        cond_rstd = reciprocal_std(cond_squares, S, "cond")
+        node_rstd = reciprocal_std(node_squares, N, "node")
 
         scratch_sigmoid = held.tile([P, 1], F32, name="scratch_sigmoid")
-        nc.scalar.activation(scratch_sigmoid[:], node_std[:, 0:1], ACT.Sigmoid)
+        nc.scalar.activation(scratch_sigmoid[:], node_rstd[:, 0:1], ACT.Sigmoid)
 
-        cond_rstd = held.tile([P, S], F32, name="cond_rstd")
-        nc.vector.reciprocal(cond_rstd[:], cond_std[:])
         cn = held.tile([P, S], BF16, name="cn")
         nc.vector.scalar_tensor_tensor(cn[:], cond_centred[:], ln_w_sb[:, 0:1], cond_rstd[:], MULT, MULT)
 
@@ -84,8 +82,6 @@ def tile_conditionedblockattentionpairbias_kernel(tc, node, cond, ln_w, w, b, of
         tab = held.tile([P, S], F32, name="tab")
         nc.scalar.activation(tab[:], projected[:], ACT.Sigmoid, bias=b_sb[:, 0:1])
 
-        node_rstd = held.tile([P, N], F32, name="node_rstd")
-        nc.vector.reciprocal(node_rstd[:], node_std[:])
         sn = held.tile([P, N], F32, name="sn")
         nc.vector.tensor_tensor(sn[:], node_centred[:], node_rstd[:], MULT)
 

@@ -10,6 +10,7 @@ P = 128
 S = 256
 N = 128
 EPS = 1e-5
+WARM_UP = 8
 
 FLOPS = 2 * P * P * S
 
@@ -32,6 +33,12 @@ def tile_conditionedblockattentionpairbias_kernel(tc, node, cond, ln_w, w, b, of
         nc.sync.dma_start(b_sb[:], b)
         offsets = held.tile([P, N // 16], U16, name="offsets")
         nc.sync.dma_start(offsets[:], offs)
+
+        zeros = held.tile([P, S], BF16, name="zeros")
+        nc.gpsimd.memset(zeros[:], 0.0)
+        unused = psum.tile([P, S], F32, name="unused")
+        for repeat in range(WARM_UP):
+            nc.tensor.matmul(unused[:], zeros[:, 0:P], zeros[:], start=True, stop=True)
 
         centre = held.tile([P, P], F32, name="centre")
         nc.gpsimd.memset(centre[:], -1.0 / P)

@@ -5,6 +5,7 @@ BF16 = mybir.dt.bfloat16
 U16 = mybir.dt.uint16
 ACT = mybir.ActivationFunctionType
 MULT = mybir.AluOpType.mult
+ADD = mybir.AluOpType.add
 
 P = 128
 S = 256
@@ -21,12 +22,16 @@ def tile_conditionedblockattentionpairbias_kernel(tc, node, cond, ln_w, w, b, of
         tc.tile_pool(name="held", bufs=1) as held,
         tc.psum_pool(name="psum", bufs=1) as psum,
     ):
-        cond_sb = held.tile([P, S], F32, name="cond_sb")
-        nc.sync.dma_start(cond_sb[:], cond)
-        node_sb = held.tile([P, N], F32, name="node_sb")
-        nc.scalar.dma_start(node_sb[:], node)
+        blocks = (cond[:, 0:P], cond[:, P:S], node)
+        NODE = 2
+        numbers = range(len(blocks))
+
+        raw = [held.tile([P, P], F32, name="raw" + str(i)) for i in numbers]
+        for i in numbers:
+            queue = nc.sync if i % 2 == 0 else nc.scalar
+            queue.dma_start(raw[i][:], blocks[i])
         ln_w_sb = held.tile([P, 1], F32, name="ln_w_sb")
-        nc.sync.dma_start(ln_w_sb[:], ln_w)
+        nc.scalar.dma_start(ln_w_sb[:], ln_w)
         w_sb = held.tile([P, P], BF16, name="w_sb")
         nc.scalar.dma_start(w_sb[:], w)
         b_sb = held.tile([P, 1], F32, name="b_sb")
@@ -59,38 +64,40 @@ def tile_conditionedblockattentionpairbias_kernel(tc, node, cond, ln_w, w, b, of
         scratch_rsqrt = held.tile([P, 1], F32, name="scratch_rsqrt")
         nc.scalar.activation(scratch_rsqrt[:], scratch[:], ACT.Abs_reciprocal_sqrt)
 
-        def centred_squares(x_sb, width, name):
-            centred = psum.tile([P, width], F32, name=name + "_centred")
-            nc.tensor.matmul(centred[:], centre[:], x_sb[:], start=True, stop=True)
-            squares = held.tile([P, width], F32, name=name + "_squares")
-            nc.scalar.activation(squares[:], centred[:], ACT.Square)
-            return centred, squares
-
-        def reciprocal_std(squares, width, name):
-            var = psum.tile([P, width], F32, name=name + "_var")
-            nc.tensor.matmul(var[:], average[:], squares[:], start=True, stop=True)
-            rstd = held.tile([P, width], F32, name=name + "_rstd")
-            nc.scalar.activation(rstd[:], var[:], ACT.Abs_reciprocal_sqrt, bias=EPS)
-            return rstd
-
-        cond_centred, cond_squares = centred_squares(cond_sb, S, "cond")
-        node_centred, node_squares = centred_squares(node_sb, N, "node")
-        cond_rstd = reciprocal_std(cond_squares, S, "cond")
-        node_rstd = reciprocal_std(node_squares, N, "node")
-
-        scratch_sigmoid = held.tile([P, 1], F32, name="scratch_sigmoid")
-        nc.scalar.activation(scratch_sigmoid[:], node_rstd[:, 0:1], ACT.Sigmoid)
+        centred = [psum.tile([P, P], F32, name="centred" + str(i)) for i in numbers]
+        for i in numbers:
+            nc.tensor.matmul(centred[i][:], centre[:], raw[i][:], start=True, stop=True)
+        squares = [held.tile([P, P], F32, name="squares" + str(i)) for i in numbers]
+        for i in numbers:
+            nc.scalar.activation(squares[i][:], centred[i][:], ACT.Square)
+        var = [psum.tile([P, P], F32, name="var" + str(i)) for i in numbers]
+        for i in numbers:
+            nc.tensor.matmul(var[i][:], average[:], squares[i][:], start=True, stop=True)
+        rstd = [held.tile([P, P], F32, name="rstd" + str(i)) for i in numbers]
+        for i in numbers:
+            nc.scalar.activation(rstd[i][:], var[i][:], ACT.Abs_reciprocal_sqrt, bias=EPS)
 
         cn = held.tile([P, S], BF16, name="cn")
-        nc.vector.scalar_tensor_tensor(cn[:], cond_centred[:], ln_w_sb[:, 0:1], cond_rstd[:], MULT, MULT)
+        for i in range(NODE):
+            nc.vector.scalar_tensor_tensor(
+                cn[:, i * P : (i + 1) * P], centred[i][:], ln_w_sb[:, 0:1], rstd[i][:], MULT, MULT
+            )
 
         projected = psum.tile([P, S], F32, name="projected")
         nc.tensor.matmul(projected[:], w_sb[:], cn[:], start=True, stop=True)
         tab = held.tile([P, S], F32, name="tab")
         nc.scalar.activation(tab[:], projected[:], ACT.Sigmoid, bias=b_sb[:, 0:1])
 
+        r_squared = held.tile([P, N], F32, name="r_squared")
+        nc.vector.tensor_tensor(r_squared[:], rstd[NODE][:], rstd[NODE][:], MULT)
+        near_one = held.tile([P, N], F32, name="near_one")
+        nc.vector.scalar_tensor_tensor(near_one[:], var[NODE][:], EPS, r_squared[:], ADD, MULT)
+        correction = held.tile([P, N], F32, name="correction")
+        nc.vector.tensor_scalar(correction[:], near_one[:], -0.5, 1.5, MULT, ADD)
+        sn_rough = held.tile([P, N], F32, name="sn_rough")
+        nc.vector.tensor_tensor(sn_rough[:], centred[NODE][:], rstd[NODE][:], MULT)
         sn = held.tile([P, N], F32, name="sn")
-        nc.vector.tensor_tensor(sn[:], node_centred[:], node_rstd[:], MULT)
+        nc.vector.tensor_tensor(sn[:], sn_rough[:], correction[:], MULT)
 
         product = held.tile([P, N], F32, name="product")
         nc.vector.tensor_tensor(product[:], tab[:].indirect(offsets[:]), sn[:], MULT)

@@ -11,7 +11,7 @@ P = 128
 S = 256
 N = 128
 EPS = 1e-5
-WARM_UP = 8
+WARM_UP = 5
 
 FLOPS = 2 * P * P * S
 

@@ -11,6 +11,7 @@ P = 128
 S = 256
 N = 128
 EPS = 1e-5
+
 WARM_UP = 5
 
 FLOPS = 2 * P * P * S
@@ -23,11 +24,12 @@ def tile_conditionedblockattentionpairbias_kernel(tc, node, cond, ln_w, w, b, of
         tc.psum_pool(name="psum", bufs=1) as psum,
     ):
         blocks = (cond[:, 0:P], cond[:, P:S], node)
-        NODE = 2
-        numbers = range(len(blocks))
+        block_ids = range(len(blocks))
+        cond_ids = range(S // P)
+        node_id = S // P
 
-        raw = [held.tile([P, P], F32, name="raw" + str(i)) for i in numbers]
-        for i in numbers:
+        raw = [held.tile([P, P], F32, name="raw" + str(i)) for i in block_ids]
+        for i in block_ids:
             queue = nc.sync if i % 2 == 0 else nc.scalar
             queue.dma_start(raw[i][:], blocks[i])
         ln_w_sb = held.tile([P, 1], F32, name="ln_w_sb")
@@ -41,9 +43,9 @@ def tile_conditionedblockattentionpairbias_kernel(tc, node, cond, ln_w, w, b, of
 
         zeros = held.tile([P, S], BF16, name="zeros")
         nc.gpsimd.memset(zeros[:], 0.0)
-        unused = psum.tile([P, S], F32, name="unused")
+        warm_up_out = psum.tile([P, S], F32, name="warm_up_out")
         for repeat in range(WARM_UP):
-            nc.tensor.matmul(unused[:], zeros[:, 0:P], zeros[:], start=True, stop=True)
+            nc.tensor.matmul(warm_up_out[:], zeros[:, 0:P], zeros[:], start=True, stop=True)
 
         centre = held.tile([P, P], F32, name="centre")
         nc.gpsimd.memset(centre[:], -1.0 / P)
@@ -64,21 +66,21 @@ def tile_conditionedblockattentionpairbias_kernel(tc, node, cond, ln_w, w, b, of
         scratch_rsqrt = held.tile([P, 1], F32, name="scratch_rsqrt")
         nc.scalar.activation(scratch_rsqrt[:], scratch[:], ACT.Abs_reciprocal_sqrt)
 
-        centred = [psum.tile([P, P], F32, name="centred" + str(i)) for i in numbers]
-        for i in numbers:
+        centred = [psum.tile([P, P], F32, name="centred" + str(i)) for i in block_ids]
+        for i in block_ids:
             nc.tensor.matmul(centred[i][:], centre[:], raw[i][:], start=True, stop=True)
-        squares = [held.tile([P, P], F32, name="squares" + str(i)) for i in numbers]
-        for i in numbers:
+        squares = [held.tile([P, P], F32, name="squares" + str(i)) for i in block_ids]
+        for i in block_ids:
             nc.scalar.activation(squares[i][:], centred[i][:], ACT.Square)
-        var = [psum.tile([P, P], F32, name="var" + str(i)) for i in numbers]
-        for i in numbers:
+        var = [psum.tile([P, P], F32, name="var" + str(i)) for i in block_ids]
+        for i in block_ids:
             nc.tensor.matmul(var[i][:], average[:], squares[i][:], start=True, stop=True)
-        rstd = [held.tile([P, P], F32, name="rstd" + str(i)) for i in numbers]
-        for i in numbers:
+        rstd = [held.tile([P, P], F32, name="rstd" + str(i)) for i in block_ids]
+        for i in block_ids:
             nc.scalar.activation(rstd[i][:], var[i][:], ACT.Abs_reciprocal_sqrt, bias=EPS)
 
         cn = held.tile([P, S], BF16, name="cn")
-        for i in range(NODE):
+        for i in cond_ids:
             nc.vector.scalar_tensor_tensor(
                 cn[:, i * P : (i + 1) * P], centred[i][:], ln_w_sb[:, 0:1], rstd[i][:], MULT, MULT
             )
@@ -88,14 +90,15 @@ def tile_conditionedblockattentionpairbias_kernel(tc, node, cond, ln_w, w, b, of
         tab = held.tile([P, S], F32, name="tab")
         nc.scalar.activation(tab[:], projected[:], ACT.Sigmoid, bias=b_sb[:, 0:1])
 
-        r_squared = held.tile([P, N], F32, name="r_squared")
-        nc.vector.tensor_tensor(r_squared[:], rstd[NODE][:], rstd[NODE][:], MULT)
+        r = rstd[node_id]
+        near_std = held.tile([P, N], F32, name="near_std")
+        nc.vector.scalar_tensor_tensor(near_std[:], var[node_id][:], EPS, r[:], ADD, MULT)
         near_one = held.tile([P, N], F32, name="near_one")
-        nc.vector.scalar_tensor_tensor(near_one[:], var[NODE][:], EPS, r_squared[:], ADD, MULT)
+        nc.vector.tensor_tensor(near_one[:], near_std[:], r[:], MULT)
         correction = held.tile([P, N], F32, name="correction")
         nc.vector.tensor_scalar(correction[:], near_one[:], -0.5, 1.5, MULT, ADD)
         sn_rough = held.tile([P, N], F32, name="sn_rough")
-        nc.vector.tensor_tensor(sn_rough[:], centred[NODE][:], rstd[NODE][:], MULT)
+        nc.vector.tensor_tensor(sn_rough[:], centred[node_id][:], r[:], MULT)
         sn = held.tile([P, N], F32, name="sn")
         nc.vector.tensor_tensor(sn[:], sn_rough[:], correction[:], MULT)
 

@@ -1,4 +1,5 @@
 import concourse.mybir as mybir
+from concourse.masks import make_identity
 
 F32 = mybir.dt.float32
 BF16 = mybir.dt.bfloat16
@@ -6,11 +7,14 @@ U16 = mybir.dt.uint16
 ACT = mybir.ActivationFunctionType
 MULT = mybir.AluOpType.mult
 ADD = mybir.AluOpType.add
+SUBTRACT = mybir.AluOpType.subtract
 
 P = 128
 S = 256
 N = 128
 EPS = 1e-5
+BN_STATS_DIM = 6
+BN_AGGR_DIM = 2
 
 WARM_UP = 5
 
@@ -23,15 +27,13 @@ def tile_conditionedblockattentionpairbias_kernel(tc, node, cond, ln_w, w, b, of
         tc.tile_pool(name="held", bufs=1) as held,
         tc.psum_pool(name="psum", bufs=1) as psum,
     ):
-        blocks = (cond[:, 0:P], cond[:, P:S], node)
-        block_ids = range(len(blocks))
-        cond_ids = range(S // P)
-        node_id = S // P
+        halves = range(S // P)
 
-        raw = [held.tile([P, P], F32, name="raw" + str(i)) for i in block_ids]
-        for i in block_ids:
-            queue = nc.sync if i % 2 == 0 else nc.scalar
-            queue.dma_start(raw[i][:], blocks[i])
+        node_raw = held.tile([P, N], F32, name="node_raw")
+        nc.sync.dma_start(node_raw[:], node)
+        cond_raw = [held.tile([P, P], F32, name="cond_raw" + str(h)) for h in halves]
+        nc.scalar.dma_start(cond_raw[0][:], cond[:, 0:P])
+        nc.sync.dma_start(cond_raw[1][:], cond[:, P:S])
         ln_w_sb = held.tile([P, 1], F32, name="ln_w_sb")
         nc.scalar.dma_start(ln_w_sb[:], ln_w)
         w_sb = held.tile([P, P], BF16, name="w_sb")
@@ -42,65 +44,76 @@ def tile_conditionedblockattentionpairbias_kernel(tc, node, cond, ln_w, w, b, of
         nc.sync.dma_start(offsets[:], offs)
 
         zeros = held.tile([P, S], BF16, name="zeros")
-        nc.gpsimd.memset(zeros[:], 0.0)
+        nc.vector.memset(zeros[:], 0.0)
         warm_up_out = psum.tile([P, S], F32, name="warm_up_out")
         for repeat in range(WARM_UP):
             nc.tensor.matmul(warm_up_out[:], zeros[:, 0:P], zeros[:], start=True, stop=True)
 
+        identity = held.tile([P, P], F32, name="identity")
+        make_identity(nc, identity[:])
         centre = held.tile([P, P], F32, name="centre")
-        nc.gpsimd.memset(centre[:], -1.0 / P)
-        nc.gpsimd.affine_select(
-            out=centre[:],
-            in_=centre[:],
-            pattern=[[-1, P]],
-            compare_op=mybir.AluOpType.not_equal,
-            fill=1.0 - 1.0 / P,
-            base=0,
-            channel_multiplier=1,
-        )
-        average = held.tile([P, P], F32, name="average")
-        nc.vector.memset(average[:], 1.0 / P)
+        nc.vector.tensor_scalar_add(centre[:], identity[:], -1.0 / P)
 
         scratch = held.tile([P, 1], F32, name="scratch")
         nc.vector.memset(scratch[:], 1.0)
         scratch_rsqrt = held.tile([P, 1], F32, name="scratch_rsqrt")
         nc.scalar.activation(scratch_rsqrt[:], scratch[:], ACT.Abs_reciprocal_sqrt)
 
-        centred = [psum.tile([P, P], F32, name="centred" + str(i)) for i in block_ids]
-        for i in block_ids:
-            nc.tensor.matmul(centred[i][:], centre[:], raw[i][:], start=True, stop=True)
-        squares = [held.tile([P, P], F32, name="squares" + str(i)) for i in block_ids]
-        for i in block_ids:
-            nc.scalar.activation(squares[i][:], centred[i][:], ACT.Square)
-        var = [psum.tile([P, P], F32, name="var" + str(i)) for i in block_ids]
-        for i in block_ids:
-            nc.tensor.matmul(var[i][:], average[:], squares[i][:], start=True, stop=True)
-        rstd = [held.tile([P, P], F32, name="rstd" + str(i)) for i in block_ids]
-        for i in block_ids:
-            nc.scalar.activation(rstd[i][:], var[i][:], ACT.Abs_reciprocal_sqrt, bias=EPS)
+        node_flipped = psum.tile([P, P], F32, name="node_flipped")
+        nc.tensor.transpose(node_flipped[:], node_raw[:], identity[:])
+        cond_flipped = [psum.tile([P, P], F32, name="cond_flipped" + str(h)) for h in halves]
+        for h in halves:
+            nc.tensor.transpose(cond_flipped[h][:], cond_raw[h][:], identity[:])
 
-        cn = held.tile([P, S], BF16, name="cn")
-        for i in cond_ids:
-            nc.vector.scalar_tensor_tensor(
-                cn[:, i * P : (i + 1) * P], centred[i][:], ln_w_sb[:, 0:1], rstd[i][:], MULT, MULT
-            )
+        node_stats = held.tile([P, BN_STATS_DIM], F32, name="node_stats")
+        cond_stats = [held.tile([P, BN_STATS_DIM], F32, name="cond_stats" + str(h)) for h in halves]
+        node_mean_var = held.tile([P, BN_AGGR_DIM], F32, name="node_mean_var")
+        cond_mean_var = held.tile([P, S // P, BN_AGGR_DIM], F32, name="cond_mean_var")
+        nc.vector.bn_stats(node_stats[:], node_flipped[:])
+        nc.vector.bn_stats(cond_stats[0][:], cond_flipped[0][:])
+        nc.vector.bn_aggr(node_mean_var[:], node_stats[:])
+        nc.vector.bn_stats(cond_stats[1][:], cond_flipped[1][:])
+        for h in halves:
+            nc.vector.bn_aggr(cond_mean_var[:, h, :], cond_stats[h][:])
+        node_mean = node_mean_var[:, 0:1]
+        node_var = node_mean_var[:, 1:2]
 
-        projected = psum.tile([P, S], F32, name="projected")
-        nc.tensor.matmul(projected[:], w_sb[:], cn[:], start=True, stop=True)
+        node_r = held.tile([P, 1], F32, name="node_r")
+        nc.scalar.activation(node_r[:], node_var, ACT.Abs_reciprocal_sqrt, bias=EPS)
+        near_std = held.tile([P, 1], F32, name="near_std")
+        nc.vector.scalar_tensor_tensor(near_std[:], node_var, EPS, node_r[:], ADD, MULT)
+        minus_half = held.tile([P, 1], F32, name="minus_half")
+        nc.vector.scalar_tensor_tensor(minus_half[:], near_std[:], -0.5, node_r[:], MULT, MULT)
+        node_rstd = held.tile([P, 1], F32, name="node_rstd")
+        nc.vector.scalar_tensor_tensor(node_rstd[:], minus_half[:], 1.5, node_r[:], ADD, MULT)
+
+        centred = [psum.tile([P, P], F32, name="centred" + str(h)) for h in halves]
+        for h in halves:
+            nc.tensor.matmul(centred[h][:], centre[:], cond_raw[h][:], start=True, stop=True)
+        gained = [held.tile([P, P], BF16, name="gained" + str(h)) for h in halves]
+        for h in halves:
+            nc.scalar.activation(gained[h][:], centred[h][:], ACT.Copy, scale=ln_w_sb[:, 0:1])
+
+        cond_rstd = held.tile([P, S // P], F32, name="cond_rstd")
+        nc.scalar.activation(cond_rstd[:], cond_mean_var[:, :, 1], ACT.Abs_reciprocal_sqrt, bias=EPS)
+
+        projected = psum.tile([P, S], F32, name="projected", tag="cond_flipped0")
+        for h in halves:
+            unscaled = psum.tile([P, P], F32, name="unscaled" + str(h))
+            nc.tensor.matmul(unscaled[:], gained[h][:], w_sb[:], start=True, stop=True)
+            scaled = held.tile([P, P], F32, name="scaled" + str(h))
+            nc.vector.tensor_scalar_mul(scaled[:], unscaled[:], cond_rstd[:, h : h + 1])
+            nc.tensor.transpose(projected[:, h * P : (h + 1) * P], scaled[:], identity[:])
+
+        sn_flipped = held.tile([P, P], F32, name="sn_flipped")
+        nc.vector.tensor_scalar(sn_flipped[:], node_flipped[:], node_mean, node_rstd[:, 0:1], SUBTRACT, MULT)
+        sn_psum = psum.tile([P, N], F32, name="sn_psum", tag="cond_flipped1")
+        nc.tensor.transpose(sn_psum[:], sn_flipped[:], identity[:])
+        sn = held.tile([P, N], F32, name="sn")
+        nc.vector.tensor_copy(sn[:], sn_psum[:])
+
         tab = held.tile([P, S], F32, name="tab")
         nc.scalar.activation(tab[:], projected[:], ACT.Sigmoid, bias=b_sb[:, 0:1])
-
-        r = rstd[node_id]
-        near_std = held.tile([P, N], F32, name="near_std")
-        nc.vector.scalar_tensor_tensor(near_std[:], var[node_id][:], EPS, r[:], ADD, MULT)
-        near_one = held.tile([P, N], F32, name="near_one")
-        nc.vector.tensor_tensor(near_one[:], near_std[:], r[:], MULT)
-        correction = held.tile([P, N], F32, name="correction")
-        nc.vector.tensor_scalar(correction[:], near_one[:], -0.5, 1.5, MULT, ADD)
-        sn_rough = held.tile([P, N], F32, name="sn_rough")
-        nc.vector.tensor_tensor(sn_rough[:], centred[node_id][:], r[:], MULT)
-        sn = held.tile([P, N], F32, name="sn")
-        nc.vector.tensor_tensor(sn[:], sn_rough[:], correction[:], MULT)
 
         product = held.tile([P, N], F32, name="product")
         nc.vector.tensor_tensor(product[:], tab[:].indirect(offsets[:]), sn[:], MULT)

@@ -32,12 +32,12 @@ def tile_conditionedblockattentionpairbias_kernel(tc, node, cond, ln_w, w, b, of
         node_raw = held.tile([P, N], F32, name="node_raw")
         nc.sync.dma_start(node_raw[:], node)
         cond_raw = [held.tile([P, P], F32, name="cond_raw" + str(h)) for h in halves]
-        nc.scalar.dma_start(cond_raw[0][:], cond[:, 0:P])
-        nc.sync.dma_start(cond_raw[1][:], cond[:, P:S])
+        for h in halves:
+            nc.sync.dma_start(cond_raw[h][:], cond[:, h * P : (h + 1) * P])
         ln_w_sb = held.tile([P, 1], F32, name="ln_w_sb")
-        nc.scalar.dma_start(ln_w_sb[:], ln_w)
+        nc.sync.dma_start(ln_w_sb[:], ln_w)
         w_sb = held.tile([P, P], BF16, name="w_sb")
-        nc.scalar.dma_start(w_sb[:], w)
+        nc.sync.dma_start(w_sb[:], w)
         b_sb = held.tile([P, 1], F32, name="b_sb")
         nc.sync.dma_start(b_sb[:], b)
         offsets = held.tile([P, N // 16], U16, name="offsets")

import concourse.mybir as mybir
from concourse.masks import make_identity

F32 = mybir.dt.float32
BF16 = mybir.dt.bfloat16
U16 = mybir.dt.uint16
ACT = mybir.ActivationFunctionType
MULT = mybir.AluOpType.mult
ADD = mybir.AluOpType.add
SUBTRACT = mybir.AluOpType.subtract

P = 128
S = 256
N = 128
EPS = 1e-5
BN_STATS_DIM = 6
BN_AGGR_DIM = 2

WARM_UP = 5

FLOPS = 2 * P * P * S


def tile_conditionedblockattentionpairbias_kernel(tc, node, cond, ln_w, w, b, offs, out):
    nc = tc.nc
    with (
        tc.tile_pool(name="held", bufs=1) as held,
        tc.psum_pool(name="psum", bufs=1) as psum,
    ):
        halves = range(S // P)

        node_raw = held.tile([P, N], F32, name="node_raw")
        nc.sync.dma_start(node_raw[:], node)
        cond_raw = [held.tile([P, P], F32, name="cond_raw" + str(h)) for h in halves]
        for h in halves:
            nc.sync.dma_start(cond_raw[h][:], cond[:, h * P : (h + 1) * P])
        ln_w_sb = held.tile([P, 1], F32, name="ln_w_sb")
        nc.sync.dma_start(ln_w_sb[:], ln_w)
        w_sb = held.tile([P, P], BF16, name="w_sb")
        nc.sync.dma_start(w_sb[:], w)
        b_sb = held.tile([P, 1], F32, name="b_sb")
        nc.sync.dma_start(b_sb[:], b)
        offsets = held.tile([P, N // 16], U16, name="offsets")
        nc.sync.dma_start(offsets[:], offs)

        zeros = held.tile([P, S], BF16, name="zeros")
        nc.vector.memset(zeros[:], 0.0)
        warm_up_out = psum.tile([P, S], F32, name="warm_up_out")
        for repeat in range(WARM_UP):
            nc.tensor.matmul(warm_up_out[:], zeros[:, 0:P], zeros[:], start=True, stop=True)

        identity = held.tile([P, P], F32, name="identity")
        make_identity(nc, identity[:])
        centre = held.tile([P, P], F32, name="centre")
        nc.vector.tensor_scalar_add(centre[:], identity[:], -1.0 / P)

        scratch = held.tile([P, 1], F32, name="scratch")
        nc.vector.memset(scratch[:], 1.0)
        scratch_rsqrt = held.tile([P, 1], F32, name="scratch_rsqrt")
        nc.scalar.activation(scratch_rsqrt[:], scratch[:], ACT.Abs_reciprocal_sqrt)

        node_flipped = psum.tile([P, P], F32, name="node_flipped")
        nc.tensor.transpose(node_flipped[:], node_raw[:], identity[:])
        cond_flipped = [psum.tile([P, P], F32, name="cond_flipped" + str(h)) for h in halves]
        for h in halves:
            nc.tensor.transpose(cond_flipped[h][:], cond_raw[h][:], identity[:])

        node_stats = held.tile([P, BN_STATS_DIM], F32, name="node_stats")
        cond_stats = [held.tile([P, BN_STATS_DIM], F32, name="cond_stats" + str(h)) for h in halves]
        node_mean_var = held.tile([P, BN_AGGR_DIM], F32, name="node_mean_var")
        cond_mean_var = held.tile([P, S // P, BN_AGGR_DIM], F32, name="cond_mean_var")
        nc.vector.bn_stats(node_stats[:], node_flipped[:])
        nc.vector.bn_stats(cond_stats[0][:], cond_flipped[0][:])
        nc.vector.bn_aggr(node_mean_var[:], node_stats[:])
        nc.vector.bn_stats(cond_stats[1][:], cond_flipped[1][:])
        for h in halves:
            nc.vector.bn_aggr(cond_mean_var[:, h, :], cond_stats[h][:])
        node_mean = node_mean_var[:, 0:1]
        node_var = node_mean_var[:, 1:2]

        node_r = held.tile([P, 1], F32, name="node_r")
        nc.scalar.activation(node_r[:], node_var, ACT.Abs_reciprocal_sqrt, bias=EPS)
        near_std = held.tile([P, 1], F32, name="near_std")
        nc.vector.scalar_tensor_tensor(near_std[:], node_var, EPS, node_r[:], ADD, MULT)
        minus_half = held.tile([P, 1], F32, name="minus_half")
        nc.vector.scalar_tensor_tensor(minus_half[:], near_std[:], -0.5, node_r[:], MULT, MULT)
        node_rstd = held.tile([P, 1], F32, name="node_rstd")
        nc.vector.scalar_tensor_tensor(node_rstd[:], minus_half[:], 1.5, node_r[:], ADD, MULT)

        centred = [psum.tile([P, P], F32, name="centred" + str(h)) for h in halves]
        for h in halves:
            nc.tensor.matmul(centred[h][:], centre[:], cond_raw[h][:], start=True, stop=True)
        gained = [held.tile([P, P], BF16, name="gained" + str(h)) for h in halves]
        for h in halves:
            nc.scalar.activation(gained[h][:], centred[h][:], ACT.Copy, scale=ln_w_sb[:, 0:1])

        cond_rstd = held.tile([P, S // P], F32, name="cond_rstd")
        nc.scalar.activation(cond_rstd[:], cond_mean_var[:, :, 1], ACT.Abs_reciprocal_sqrt, bias=EPS)

        projected = psum.tile([P, S], F32, name="projected", tag="cond_flipped0")
        for h in halves:
            unscaled = psum.tile([P, P], F32, name="unscaled" + str(h))
            nc.tensor.matmul(unscaled[:], gained[h][:], w_sb[:], start=True, stop=True)
            scaled = held.tile([P, P], F32, name="scaled" + str(h))
            nc.vector.tensor_scalar_mul(scaled[:], unscaled[:], cond_rstd[:, h : h + 1])
            nc.tensor.transpose(projected[:, h * P : (h + 1) * P], scaled[:], identity[:])

        sn_flipped = held.tile([P, P], F32, name="sn_flipped")
        nc.vector.tensor_scalar(sn_flipped[:], node_flipped[:], node_mean, node_rstd[:, 0:1], SUBTRACT, MULT)
        sn_psum = psum.tile([P, N], F32, name="sn_psum", tag="cond_flipped1")
        nc.tensor.transpose(sn_psum[:], sn_flipped[:], identity[:])
        sn = held.tile([P, N], F32, name="sn")
        nc.vector.tensor_copy(sn[:], sn_psum[:])

        tab = held.tile([P, S], F32, name="tab")
        nc.scalar.activation(tab[:], projected[:], ACT.Sigmoid, bias=b_sb[:, 0:1])

        product = held.tile([P, N], F32, name="product")
        nc.vector.tensor_tensor(product[:], tab[:].indirect(offsets[:]), sn[:], MULT)
        nc.sync.dma_start(out, product[:])
